import numpy as np
import ml_dtypes


def mxq(x, axis, fmt="e4m3"):
    dtype, down = {"e4m3": (ml_dtypes.float8_e4m3fn, 7), "e5m2": (ml_dtypes.float8_e5m2, 14)}[fmt]
    v = np.moveaxis(np.asarray(x, np.float32).astype(ml_dtypes.bfloat16).astype(np.float64), axis, -1)
    blocks = v.reshape(v.shape[:-1] + (-1, 32))
    amax = np.abs(blocks).max(-1, keepdims=True)
    byte = np.maximum(np.where(amax > 0, np.frexp(amax)[1] - 1 + 127, 0) - down, 1)
    scale = np.exp2(byte - 127.0)
    codes = (blocks / scale).astype(np.float32).astype(dtype).astype(np.float64)
    return np.moveaxis((codes * scale).reshape(v.shape), -1, axis)


WIDE = False


def mx_kscale(k):
    if not WIDE:
        return np.ones(k)
    levels = np.array([10, -10, 5, -5, 0])
    a = np.random.permutation(np.resize(levels, k // 512 * 4)).reshape(k // 512, 4)
    idx = np.arange(k)
    return np.exp2(a[idx // 512, idx % 128 // 32])


BF16 = ml_dtypes.bfloat16


def bf(x):
    return np.asarray(x, np.float32).astype(BF16)


def f64(x):
    return np.asarray(x).astype(np.float64)


E2M1 = np.array([0.0, 0.5, 1.0, 1.5, 2.0, 3.0, 4.0, 6.0, -0.0, -0.5, -1.0, -1.5, -2.0, -3.0, -4.0, -6.0])


def pack_weight(w, fmt):
    k, n = w.shape
    w = f64(bf(w)).reshape(k // 32, 32, n)
    amax = np.abs(w).max(1)
    if fmt == "e4m3":
        byte = np.frexp(amax)[1] - 1 + 127 - 7
    else:
        mant, ex = np.frexp(amax / 6.0)
        byte = np.where(mant > 0.5, ex, ex - 1) + 127
    byte = np.clip(np.where(amax > 0, byte, 1), 1, 254)
    scaled = (w * np.exp2(127.0 - byte)[:, None, :]).reshape(k, n).astype(np.float32)
    by_word = np.ascontiguousarray(scaled.reshape(k // 512, 128, 4, n).transpose(0, 1, 3, 2))
    if fmt == "e4m3":
        words = by_word.astype(ml_dtypes.float8_e4m3fn).view(np.uint8)
    else:
        c = by_word.astype(ml_dtypes.float4_e2m1fn).view(np.uint8) & 0xF
        words = c[..., 0::2] | (c[..., 1::2] << 4)
    return np.ascontiguousarray(words), np.ascontiguousarray(byte.astype(np.uint8).reshape(k // 512, 16, n))


def unpack_weight(words, scales, fmt):
    g, p, n, _ = words.shape
    if fmt == "e4m3":
        vals = np.ascontiguousarray(words).view(ml_dtypes.float8_e4m3fn).astype(np.float64)
    else:
        nib = np.empty((g, p, n, 4), np.uint8)
        nib[..., 0::2] = words & 0xF
        nib[..., 1::2] = words >> 4
        vals = E2M1[nib]
    vals = vals * np.repeat(np.exp2(scales.astype(np.float64) - 127.0), 8, axis=1)[..., None]
    return vals.transpose(0, 1, 3, 2).reshape(g * 512, n)

def pack4(w):
    words, scales = pack_weight(w, "e2m1")
    return words.reshape(words.shape[0], 128, -1), scales


def unpack4(words, scales):
    return unpack_weight(words.reshape(words.shape[0], 128, -1, 2), scales, "e2m1")


B, L, DIM, H, D = 4, 2048, 1024, 2, 64
EPS = 1e-6
THETA = 10000.0


def rope_table(seq_len, head_dim):
    pos = np.arange(seq_len, dtype=np.float64)
    inv = 1.0 / (THETA ** (np.arange(0, head_dim, 2, dtype=np.float64) / head_dim))
    ang = pos[:, None] * inv[None, :]
    cos, sin = np.cos(ang), np.sin(ang)
    rot = np.stack([np.stack([cos, -sin], -1), np.stack([sin, cos], -1)], -2)
    return rot[None, None]


def rms_norm(u, gain):
    rrms = 1.0 / np.sqrt(np.mean(np.square(u), axis=-1, keepdims=True) + EPS)
    return u * rrms * gain


def rope(u, table):
    ur = u.reshape(*u.shape[:-1], -1, 1, 2)
    out = table[..., 0] * ur[..., 0] + table[..., 1] * ur[..., 1]
    return out.reshape(u.shape)


def setup_inputs():
    s = mx_kscale(DIM)
    x = bf(np.random.standard_normal((B, L, DIM)) * s)
    pe = bf(rope_table(L, D))
    words, scales = pack4(np.random.standard_normal((DIM, 3 * H * D)) / np.sqrt(DIM) / s[:, None])
    qkv_b = bf(np.random.standard_normal(3 * H * D) * 0.2)
    q_scale = bf(1.0 + 0.1 * np.random.standard_normal(D))
    k_scale = bf(1.0 + 0.1 * np.random.standard_normal(D))
    return {"x": x,
            "pe": pe,
            "qkv_w_words": words,
            "qkv_w_scales": scales,
            "qkv_b": qkv_b,
            "q_scale": q_scale,
            "k_scale": k_scale}


def reference(x, pe, qkv_w_words, qkv_w_scales, qkv_b, q_scale, k_scale):
    qkv = (mxq(f64(x), 2, "e4m3") @ unpack4(qkv_w_words, qkv_w_scales)) + f64(qkv_b)
    qkv = qkv.reshape(B, L, 3, H, D).transpose(2, 0, 3, 1, 4)
    q, k, v = qkv[0], qkv[1], qkv[2]
    q = rms_norm(q, f64(q_scale))
    k = rms_norm(k, f64(k_scale))
    table = f64(pe)
    return rope(q, table), rope(k, table), v

@@ -1,0 +1,290 @@
+from contextlib import ExitStack
+
+import concourse.mybir as mybir
+from concourse.masks import make_identity
+
+F32 = mybir.dt.float32
+BF16 = mybir.dt.bfloat16
+I32 = mybir.dt.int32
+U32 = mybir.dt.uint32
+U8 = mybir.dt.uint8
+FP8X4 = mybir.dt.float8_e4m3fn_x4
+FP4X4 = mybir.dt.float4_e2m1fn_x4
+ALU = mybir.AluOpType
+ACT = mybir.ActivationFunctionType
+
+P = 128
+BATCH, SEQ, DIM, HEADS, HEAD_DIM = 4, 2048, 1024, 2, 64
+EPS = 1e-6
+PAIRS = HEAD_DIM // 2
+STREAM = HEADS * HEAD_DIM
+K_PASS = 4 * P
+PASSES = DIM // K_PASS
+WORDS = K_PASS // 2
+POS = SEQ // P
+TILES = 4
+CHUNKS = POS // TILES
+GROUPS = 2 * HEADS
+
+FLOPS = 2 * BATCH * SEQ * DIM * 3 * STREAM
+
+
+def tile_selfattention_pa_t_kernel(
+    tc, x, pe, qkv_w_words, qkv_w_scales, qkv_b, q_scale, k_scale, out_0, out_1, out_2
+):
+    nc = tc.nc
+    with ExitStack() as ctx:
+        ctx.enter_context(tc.manual_schedule())
+        consts = ctx.enter_context(tc.tile_pool(name="consts", bufs=1))
+        x_pool = ctx.enter_context(tc.tile_pool(name="x_pool", bufs=4))
+        two_steps = ctx.enter_context(tc.tile_pool(name="two_steps", bufs=2))
+        three_steps = ctx.enter_context(tc.tile_pool(name="three_steps", bufs=3))
+        turn_psum = ctx.enter_context(tc.psum_pool(name="turn_psum", bufs=4))
+        qk_psum = ctx.enter_context(tc.psum_pool(name="qk_psum", bufs=3))
+        v_psum = ctx.enter_context(tc.psum_pool(name="v_psum", bufs=1))
+
+        n_chunks = BATCH * CHUNKS
+        x_tiles = {}
+        grouped_tiles = {}
+        code_tiles = {}
+        banks = {}
+        plane_tiles = {}
+        rms_tiles = {}
+        rotated_tiles = {}
+
+        def exists(n):
+            return 0 <= n < n_chunks
+
+        def batch_of(n):
+            return n // CHUNKS
+
+        def positions_of(n):
+            return slice((n % CHUNKS) * TILES, (n % CHUNKS + 1) * TILES)
+
+        def load(n):
+            x_sb = x_pool.tile([P, TILES, DIM], BF16)
+            x_rows = x[batch_of(n)].rearrange("(p j) k -> p j k", p=P)
+            nc.sync.dma_start(out=x_sb[:], in_=x_rows[:, positions_of(n), :])
+            x_tiles[n] = x_sb
+
+        def turn(n):
+            x_sb = x_tiles[n]
+            grouped = two_steps.tile([P, TILES, PASSES, P, 4], BF16, align_bytes=64)
+            for t in range(TILES):
+                x_words = x_sb[:, t, :].bitcast(F32)
+                turned = turn_psum.tile([P, PASSES, 2, P], F32)
+                for g in range(PASSES):
+                    for u in range(2):
+                        nc.tensor.transpose(
+                            turned[:, g, u, :],
+                            x_words[:, WORDS * g + u : WORDS * (g + 1) : 2],
+                            identity[:],
+                        )
+                nc.scalar.copy(
+                    out=grouped[:, t]
+                    .rearrange("p g r k -> p g (r k)")
+                    .bitcast(F32)
+                    .rearrange("p g (r u) -> p g r u", u=2),
+                    in_=turned[:].rearrange("p g u r -> p g r u"),
+                )
+            grouped_tiles[n] = grouped
+
+        def quantise(n):
+            grouped = grouped_tiles[n]
+            x_codes = two_steps.tile([P, TILES, PASSES, P], U32, align_bytes=64)
+            x_scales = two_steps.tile([P, TILES, PASSES, P], U8, align_bytes=64)
+            nc.vector.quantize_mx(
+                out=x_codes[:].rearrange("p t g r -> p (t g r)").bitcast(FP8X4),
+                scales=x_scales[:].rearrange("p t g r -> p (t g r)"),
+                in_=grouped[:].rearrange("p t g r k -> p (t g r k)"),
+            )
+            code_tiles[n] = (x_codes, x_scales)
+
+        def project(n):
+            x_codes, x_scales = code_tiles[n]
+            qk_banks = []
+            for half in range(TILES // 2):
+                qk_bank = qk_psum.tile([P, 2, 2, STREAM], F32)
+                qk_banks.append(qk_bank)
+            v_bank = v_psum.tile([P, TILES, STREAM], F32)
+            for t in range(TILES):
+                for s in range(3):
+                    if s < 2:
+                        product = qk_banks[t // 2][:, t % 2, s, :]
+                    else:
+                        product = v_bank[:, t, :]
+                    for g in range(PASSES):
+                        nc.tensor.matmul_mx(
+                            out=product,
+                            lhsT=x_codes[:, t, g, :].bitcast(FP8X4),
+                            lhsT_scale=x_scales[:, t, g, :],
+                            rhs=w_words[:, g, 2 * STREAM * s : 2 * STREAM * (s + 1)].bitcast(FP4X4),
+                            rhs_scale=w_scales[:, g, STREAM * s : STREAM * (s + 1)],
+                            start=(g == 0),
+                            stop=(g == PASSES - 1),
+                        )
+            banks[n] = (qk_banks, v_bank)
+
+        def add_bias(n):
+            qk_banks, v_bank = banks[n]
+            planes = two_steps.tile([P, GROUPS, TILES, 2, PAIRS], F32)
+            for half in range(TILES // 2):
+                nc.vector.tensor_tensor(
+                    out=planes[:, :, 2 * half : 2 * half + 2, :, :].rearrange(
+                        "p c t e i -> p t c e i"
+                    ),
+                    in0=qk_banks[half][:].rearrange("p t s (h i e) -> p t (s h) e i", h=HEADS, e=2),
+                    in1=bias_qk[:].unsqueeze(1).to_broadcast([P, 2, GROUPS, 2, PAIRS]),
+                    op=ALU.add,
+                )
+            v_sb = three_steps.tile([P, HEADS, TILES, HEAD_DIM], F32)
+            nc.vector.tensor_tensor(
+                out=v_sb[:].rearrange("p h t d -> p t h d"),
+                in0=v_bank[:].rearrange("p t (h d) -> p t h d", h=HEADS),
+                in1=bias_v[:].unsqueeze(1).to_broadcast([P, TILES, HEADS, HEAD_DIM]),
+                op=ALU.add,
+            )
+            v_rows = out_2[batch_of(n)].rearrange("h (p j) d -> p h j d", p=P)
+            nc.sync.dma_start(out=v_rows[:, :, positions_of(n), :], in_=v_sb[:])
+            plane_tiles[n] = planes
+
+        def measure(n):
+            planes = plane_tiles[n]
+            squares = two_steps.tile([P, GROUPS, TILES, 2, PAIRS], F32)
+            sum_sq = two_steps.tile([P, GROUPS, TILES], F32)
+            for c in range(GROUPS):
+                for t in range(TILES):
+                    nc.scalar.activation(
+                        out=squares[:, c, t],
+                        in_=planes[:, c, t],
+                        func=ACT.Square,
+                        accum_out=sum_sq[:, c, t : t + 1],
+                    )
+            rms = two_steps.tile([P, GROUPS, TILES], F32)
+            nc.scalar.activation(
+                out=rms[:], in_=sum_sq[:], func=ACT.Sqrt, scale=1.0 / HEAD_DIM, bias=EPS
+            )
+            rms_tiles[n] = rms
+
+        def rotate(n):
+            planes = plane_tiles[n]
+            rotated = two_steps.tile([P, GROUPS, TILES, 2, PAIRS], F32)
+            nc.vector.tensor_tensor(
+                out=rotated[:].rearrange("p (s h) t e i -> p s h (t e i)", s=2),
+                in0=planes[:].rearrange("p (s h) t e i -> p s h (t e i)", s=2),
+                in1=own[:, :, positions_of(n), :, :]
+                .rearrange("p s t e i -> p s (t e i)")
+                .unsqueeze(2)
+                .to_broadcast([P, 2, HEADS, TILES * HEAD_DIM]),
+                op=ALU.mult,
+            )
+            partner = two_steps.tile([P, GROUPS, TILES, 2, PAIRS], F32)
+            for e in range(2):
+                nc.vector.tensor_tensor(
+                    out=partner[:, :, :, e, :].rearrange("p (s h) t i -> p s h t i", s=2),
+                    in0=planes[:, :, :, 1 - e, :].rearrange("p (s h) t i -> p s h t i", s=2),
+                    in1=other[:, :, e, positions_of(n), :]
+                    .unsqueeze(2)
+                    .to_broadcast([P, 2, HEADS, TILES, PAIRS]),
+                    op=ALU.mult,
+                )
+            nc.vector.tensor_tensor(out=rotated[:], in0=rotated[:], in1=partner[:], op=ALU.add)
+            inv_rms = three_steps.tile([P, GROUPS, TILES], F32)
+            nc.vector.reciprocal(out=inv_rms[:], in_=rms_tiles[n][:])
+            rotated_tiles[n] = (rotated, inv_rms)
+
+        def finish(n):
+            rotated, inv_rms = rotated_tiles[n]
+            qk_sb = three_steps.tile([P, GROUPS, TILES, PAIRS, 2], F32)
+            for c in range(GROUPS):
+                for t in range(TILES):
+                    nc.scalar.activation(
+                        out=qk_sb[:, c, t],
+                        in_=rotated[:, c, t].rearrange("p e i -> p i e"),
+                        func=ACT.Copy,
+                        scale=inv_rms[:, c, t : t + 1],
+                    )
+            q_rows = out_0[batch_of(n)].rearrange("h (p j) d -> p h j d", p=P)
+            k_rows = out_1[batch_of(n)].rearrange("h (p j) d -> p h j d", p=P)
+            nc.sync.dma_start(
+                out=q_rows[:, :, positions_of(n), :],
+                in_=qk_sb[:, 0:HEADS].rearrange("p h t i e -> p h t (i e)"),
+            )
+            nc.sync.dma_start(
+                out=k_rows[:, :, positions_of(n), :],
+                in_=qk_sb[:, HEADS:GROUPS].rearrange("p h t i e -> p h t (i e)"),
+            )
+
+        load(0)
+        identity = consts.tile([P, P], F32)
+        make_identity(nc, identity[:])
+
+        w_words = consts.tile([P, PASSES, 2 * 3 * STREAM], U8, align_bytes=64)
+        nc.sync.dma_start(
+            out=w_words[:].bitcast(I32), in_=qkv_w_words.rearrange("g p n -> p g n").bitcast(I32)
+        )
+        w_scales = consts.tile([P, PASSES, 3 * STREAM], U8, align_bytes=64)
+        nc.vector.memset(w_scales[:].rearrange("p g n -> p (g n)").bitcast(I32), 0)
+        for quadrant in range(4):
+            nc.sync.dma_start(
+                out=w_scales[32 * quadrant : 32 * quadrant + 4, :, :].bitcast(I32),
+                in_=qkv_w_scales[:, 4 * quadrant : 4 * quadrant + 4, :]
+                .rearrange("g r n -> r g n")
+                .bitcast(I32),
+            )
+
+        bias_row = consts.tile([P, 3 * STREAM], BF16)
+        nc.scalar.dma_start(out=bias_row[:], in_=qkv_b.partition_broadcast(P))
+        gain_row = consts.tile([P, 2, HEAD_DIM], BF16)
+        nc.scalar.dma_start(out=gain_row[:, 0, :], in_=q_scale.partition_broadcast(P))
+        nc.scalar.dma_start(out=gain_row[:, 1, :], in_=k_scale.partition_broadcast(P))
+        pe_rows = consts.tile([P, POS, 4 * PAIRS], BF16)
+        nc.scalar.dma_start(
+            out=pe_rows[:], in_=pe[0, 0].rearrange("(p j) i r c -> p j (i r c)", p=P)
+        )
+
+        bias_qk = consts.tile([P, GROUPS, 2, PAIRS], F32)
+        nc.vector.tensor_copy(
+            out=bias_qk[:],
+            in_=bias_row[:, 0 : 2 * STREAM].rearrange("p (c i e) -> p c e i", c=GROUPS, e=2),
+        )
+        bias_v = consts.tile([P, HEADS, HEAD_DIM], F32)
+        nc.vector.tensor_copy(
+            out=bias_v[:], in_=bias_row[:, 2 * STREAM :].rearrange("p (h d) -> p h d", h=HEADS)
+        )
+
+        own = consts.tile([P, 2, POS, 2, PAIRS], F32)
+        other = consts.tile([P, 2, 2, POS, PAIRS], F32)
+        pe_entry = pe_rows[:].rearrange("p j (i r c) -> p j i r c", r=2, c=2)
+        gain_entry = gain_row[:].rearrange("p s (i e) -> p s i e", e=2)
+        for s in range(2):
+            for e in range(2):
+                nc.gpsimd.tensor_tensor(
+                    out=own[:, s, :, e, :],
+                    in0=pe_entry[:, :, :, e, e],
+                    in1=gain_entry[:, s, :, e].unsqueeze(1).to_broadcast([P, POS, PAIRS]),
+                    op=ALU.mult,
+                )
+                nc.gpsimd.tensor_tensor(
+                    out=other[:, s, e, :, :],
+                    in0=pe_entry[:, :, :, e, 1 - e],
+                    in1=gain_entry[:, s, :, 1 - e].unsqueeze(1).to_broadcast([P, POS, PAIRS]),
+                    op=ALU.mult,
+                )
+
+        load(1)
+        for step in range(-2, n_chunks + 1):
+            if exists(step + 4):
+                load(step + 4)
+            if exists(step + 2):
+                turn(step + 2)
+            if exists(step + 1):
+                project(step + 1)
+            if exists(step):
+                add_bias(step)
+                measure(step)
+                rotate(step)
+            if exists(step + 2):
+                quantise(step + 2)
+            if exists(step - 1):
+                finish(step - 1)

@@ -188,7 +188,7 @@ def tile_selfattention_pa_t_kernel(
                     .to_broadcast([P, 2, HEADS, TILES, PAIRS]),
                     op=ALU.mult,
                 )
-            nc.vector.tensor_tensor(out=rotated[:], in0=rotated[:], in1=partner[:], op=ALU.add)
+            nc.gpsimd.tensor_tensor(out=rotated[:], in0=rotated[:], in1=partner[:], op=ALU.add)
             inv_rms = three_steps.tile([P, GROUPS, TILES], F32)
             nc.vector.reciprocal(out=inv_rms[:], in_=rms_tiles[n][:])
             rotated_tiles[n] = (rotated, inv_rms)

@@ -23,7 +23,7 @@ PASSES = DIM // K_PASS
 WORDS = K_PASS // 2
 POS = SEQ // P
 TILES = 4
-CHUNKS = POS // TILES
+QUARTERS = POS // TILES
 GROUPS = 2 * HEADS
 
 FLOPS = 2 * BATCH * SEQ * DIM * 3 * STREAM
@@ -36,14 +36,38 @@ def tile_selfattention_pa_t_kernel(
     with ExitStack() as ctx:
         ctx.enter_context(tc.manual_schedule())
         consts = ctx.enter_context(tc.tile_pool(name="consts", bufs=1))
-        x_pool = ctx.enter_context(tc.tile_pool(name="x_pool", bufs=4))
+        x_pool = ctx.enter_context(tc.tile_pool(name="x_pool", bufs=5))
         two_steps = ctx.enter_context(tc.tile_pool(name="two_steps", bufs=2))
         three_steps = ctx.enter_context(tc.tile_pool(name="three_steps", bufs=3))
-        turn_psum = ctx.enter_context(tc.psum_pool(name="turn_psum", bufs=4))
-        qk_psum = ctx.enter_context(tc.psum_pool(name="qk_psum", bufs=3))
+        turn_psum = ctx.enter_context(tc.psum_pool(name="turn_psum", bufs=3))
+        qk_psum = ctx.enter_context(tc.psum_pool(name="qk_psum", bufs=2))
         v_psum = ctx.enter_context(tc.psum_pool(name="v_psum", bufs=1))
+        table_psum = ctx.enter_context(tc.psum_pool(name="table_psum", bufs=1))
 
-        n_chunks = BATCH * CHUNKS
+        chunks = [(0, 0, 0, 1), (0, 0, 1, 1), (0, 0, 2, 2)]
+        for quarter in range(QUARTERS):
+            for b in range(BATCH):
+                if 0 < quarter * BATCH + b < QUARTERS * BATCH - 1:
+                    chunks.append((quarter, b, 0, TILES))
+        chunks.extend(
+            [
+                (QUARTERS - 1, BATCH - 1, 0, 2),
+                (QUARTERS - 1, BATCH - 1, 2, 1),
+                (QUARTERS - 1, BATCH - 1, 3, 1),
+            ]
+        )
+
+        def exists(n):
+            return 0 <= n < len(chunks)
+
+        def opens_quarter(n):
+            return n == 0 or chunks[n][0] != chunks[n - 1][0]
+
+        def rows_of(out, n):
+            quarter, b, first, tiles = chunks[n]
+            start = quarter * TILES + first
+            return out[b].rearrange("h (p j) d -> p h j d", p=P)[:, :, start : start + tiles, :]
+
         x_tiles = {}
         grouped_tiles = {}
         code_tiles = {}
@@ -51,27 +75,24 @@ def tile_selfattention_pa_t_kernel(
         plane_tiles = {}
         rms_tiles = {}
         rotated_tiles = {}
-
-        def exists(n):
-            return 0 <= n < n_chunks
-
-        def batch_of(n):
-            return n // CHUNKS
-
-        def positions_of(n):
-            return slice((n % CHUNKS) * TILES, (n % CHUNKS + 1) * TILES)
+        inv_rms_tiles = {}
+        table_banks = {}
 
         def load(n):
-            x_sb = x_pool.tile([P, TILES, DIM], BF16)
-            x_rows = x[batch_of(n)].rearrange("(p j) k -> p j k", p=P)
-            nc.sync.dma_start(out=x_sb[:], in_=x_rows[:, positions_of(n), :])
+            quarter, b, first, tiles = chunks[n]
+            start = quarter * TILES + first
+            x_sb = x_pool.tile([P, tiles, DIM], BF16)
+            nc.sync.dma_start(
+                out=x_sb[:],
+                in_=x[b].rearrange("(p j) k -> p j k", p=P)[:, start : start + tiles, :],
+            )
             x_tiles[n] = x_sb
 
         def turn(n):
-            x_sb = x_tiles[n]
-            grouped = two_steps.tile([P, TILES, PASSES, P, 4], BF16, align_bytes=64)
-            for t in range(TILES):
-                x_words = x_sb[:, t, :].bitcast(F32)
+            tiles = chunks[n][3]
+            grouped = two_steps.tile([P, tiles, PASSES, P, 4], BF16, align_bytes=64)
+            for t in range(tiles):
+                x_words = x_tiles[n][:, t, :].bitcast(F32)
                 turned = turn_psum.tile([P, PASSES, 2, P], F32)
                 for g in range(PASSES):
                     for u in range(2):
@@ -90,24 +111,25 @@ def tile_selfattention_pa_t_kernel(
             grouped_tiles[n] = grouped
 
         def quantise(n):
-            grouped = grouped_tiles[n]
-            x_codes = two_steps.tile([P, TILES, PASSES, P], U32, align_bytes=64)
-            x_scales = two_steps.tile([P, TILES, PASSES, P], U8, align_bytes=64)
+            tiles = chunks[n][3]
+            x_codes = two_steps.tile([P, tiles, PASSES, P], U32, align_bytes=64)
+            x_scales = two_steps.tile([P, tiles, PASSES, P], U8, align_bytes=64)
             nc.vector.quantize_mx(
                 out=x_codes[:].rearrange("p t g r -> p (t g r)").bitcast(FP8X4),
                 scales=x_scales[:].rearrange("p t g r -> p (t g r)"),
-                in_=grouped[:].rearrange("p t g r k -> p (t g r k)"),
+                in_=grouped_tiles[n][:].rearrange("p t g r k -> p (t g r k)"),
             )
             code_tiles[n] = (x_codes, x_scales)
 
         def project(n):
+            tiles = chunks[n][3]
             x_codes, x_scales = code_tiles[n]
             qk_banks = []
-            for half in range(TILES // 2):
+            for pair in range((tiles + 1) // 2):
                 qk_bank = qk_psum.tile([P, 2, 2, STREAM], F32)
                 qk_banks.append(qk_bank)
             v_bank = v_psum.tile([P, TILES, STREAM], F32)
-            for t in range(TILES):
+            for t in range(tiles):
                 for s in range(3):
                     if s < 2:
                         product = qk_banks[t // 2][:, t % 2, s, :]
@@ -125,97 +147,132 @@ def tile_selfattention_pa_t_kernel(
                         )
             banks[n] = (qk_banks, v_bank)
 
+        def place_tables(quarter):
+            own_bank = table_psum.tile([P, 2, TILES, HEAD_DIM], F32)
+            nc.tensor.matmul(
+                out=own_bank[:].rearrange("p s t d -> p (s t d)"),
+                lhsT=identity[:],
+                rhs=own[:, quarter].rearrange("p s t e i -> p (s t e i)"),
+                start=True,
+                stop=True,
+            )
+            other_bank = table_psum.tile([P, 2, 2, TILES, PAIRS], F32)
+            nc.tensor.matmul(
+                out=other_bank[:].rearrange("p s e t i -> p (s e t i)"),
+                lhsT=identity[:],
+                rhs=other[:, quarter].rearrange("p s e t i -> p (s e t i)"),
+                start=True,
+                stop=True,
+            )
+            table_banks[quarter] = (own_bank, other_bank)
+
         def add_bias(n):
+            tiles = chunks[n][3]
             qk_banks, v_bank = banks[n]
-            planes = two_steps.tile([P, GROUPS, TILES, 2, PAIRS], F32)
-            for half in range(TILES // 2):
+            planes = two_steps.tile([P, GROUPS, tiles, 2, PAIRS], F32)
+            for pair in range((tiles + 1) // 2):
+                held = min(2, tiles - 2 * pair)
                 nc.vector.tensor_tensor(
-                    out=planes[:, :, 2 * half : 2 * half + 2, :, :].rearrange(
+                    out=planes[:, :, 2 * pair : 2 * pair + held, :, :].rearrange(
                         "p c t e i -> p t c e i"
                     ),
-                    in0=qk_banks[half][:].rearrange("p t s (h i e) -> p t (s h) e i", h=HEADS, e=2),
-                    in1=bias_qk[:].unsqueeze(1).to_broadcast([P, 2, GROUPS, 2, PAIRS]),
+                    in0=qk_banks[pair][:, 0:held].rearrange(
+                        "p t s (h i e) -> p t (s h) e i", h=HEADS, e=2
+                    ),
+                    in1=bias_qk[:].unsqueeze(1).to_broadcast([P, held, GROUPS, 2, PAIRS]),
                     op=ALU.add,
                 )
-            v_sb = three_steps.tile([P, HEADS, TILES, HEAD_DIM], F32)
+            v_sb = three_steps.tile([P, HEADS, tiles, HEAD_DIM], F32)
             nc.vector.tensor_tensor(
                 out=v_sb[:].rearrange("p h t d -> p t h d"),
-                in0=v_bank[:].rearrange("p t (h d) -> p t h d", h=HEADS),
-                in1=bias_v[:].unsqueeze(1).to_broadcast([P, TILES, HEADS, HEAD_DIM]),
+                in0=v_bank[:, 0:tiles, :].rearrange("p t (h d) -> p t h d", h=HEADS),
+                in1=bias_v[:].unsqueeze(1).to_broadcast([P, tiles, HEADS, HEAD_DIM]),
                 op=ALU.add,
             )
-            v_rows = out_2[batch_of(n)].rearrange("h (p j) d -> p h j d", p=P)
-            nc.sync.dma_start(out=v_rows[:, :, positions_of(n), :], in_=v_sb[:])
+            nc.sync.dma_start(out=rows_of(out_2, n), in_=v_sb[:])
             plane_tiles[n] = planes
 
         def measure(n):
-            planes = plane_tiles[n]
-            squares = two_steps.tile([P, GROUPS, TILES, 2, PAIRS], F32)
-            sum_sq = two_steps.tile([P, GROUPS, TILES], F32)
+            tiles = chunks[n][3]
+            squares = two_steps.tile([P, GROUPS, tiles, 2, PAIRS], F32)
+            sum_sq = two_steps.tile([P, GROUPS, tiles], F32)
             for c in range(GROUPS):
-                for t in range(TILES):
+                for t in range(tiles):
                     nc.scalar.activation(
                         out=squares[:, c, t],
-                        in_=planes[:, c, t],
+                        in_=plane_tiles[n][:, c, t],
                         func=ACT.Square,
                         accum_out=sum_sq[:, c, t : t + 1],
                     )
-            rms = two_steps.tile([P, GROUPS, TILES], F32)
+            rms = two_steps.tile([P, GROUPS, tiles], F32)
             nc.scalar.activation(
                 out=rms[:], in_=sum_sq[:], func=ACT.Sqrt, scale=1.0 / HEAD_DIM, bias=EPS
             )
             rms_tiles[n] = rms
 
         def rotate(n):
+            quarter, b, first, tiles = chunks[n]
             planes = plane_tiles[n]
-            rotated = two_steps.tile([P, GROUPS, TILES, 2, PAIRS], F32)
+            own_bank, other_bank = table_banks[quarter]
+            rotated = three_steps.tile([P, GROUPS, tiles, 2, PAIRS], F32)
             nc.vector.tensor_tensor(
                 out=rotated[:].rearrange("p (s h) t e i -> p s h (t e i)", s=2),
                 in0=planes[:].rearrange("p (s h) t e i -> p s h (t e i)", s=2),
-                in1=own[:, :, positions_of(n), :, :]
-                .rearrange("p s t e i -> p s (t e i)")
+                in1=own_bank[:, :, first : first + tiles, :]
+                .rearrange("p s t d -> p s (t d)")
                 .unsqueeze(2)
-                .to_broadcast([P, 2, HEADS, TILES * HEAD_DIM]),
+                .to_broadcast([P, 2, HEADS, tiles * HEAD_DIM]),
                 op=ALU.mult,
             )
-            partner = two_steps.tile([P, GROUPS, TILES, 2, PAIRS], F32)
+            partner = two_steps.tile([P, GROUPS, tiles, 2, PAIRS], F32)
             for e in range(2):
                 nc.vector.tensor_tensor(
                     out=partner[:, :, :, e, :].rearrange("p (s h) t i -> p s h t i", s=2),
                     in0=planes[:, :, :, 1 - e, :].rearrange("p (s h) t i -> p s h t i", s=2),
-                    in1=other[:, :, e, positions_of(n), :]
+                    in1=other_bank[:, :, e, first : first + tiles, :]
                     .unsqueeze(2)
-                    .to_broadcast([P, 2, HEADS, TILES, PAIRS]),
+                    .to_broadcast([P, 2, HEADS, tiles, PAIRS]),
                     op=ALU.mult,
                 )
             nc.gpsimd.tensor_tensor(out=rotated[:], in0=rotated[:], in1=partner[:], op=ALU.add)
-            inv_rms = three_steps.tile([P, GROUPS, TILES], F32)
-            nc.vector.reciprocal(out=inv_rms[:], in_=rms_tiles[n][:])
-            rotated_tiles[n] = (rotated, inv_rms)
+            rotated_tiles[n] = rotated
 
-        def finish(n):
-            rotated, inv_rms = rotated_tiles[n]
-            qk_sb = three_steps.tile([P, GROUPS, TILES, PAIRS, 2], F32)
-            for c in range(GROUPS):
-                for t in range(TILES):
-                    nc.scalar.activation(
-                        out=qk_sb[:, c, t],
-                        in_=rotated[:, c, t].rearrange("p e i -> p i e"),
-                        func=ACT.Copy,
-                        scale=inv_rms[:, c, t : t + 1],
-                    )
-            q_rows = out_0[batch_of(n)].rearrange("h (p j) d -> p h j d", p=P)
-            k_rows = out_1[batch_of(n)].rearrange("h (p j) d -> p h j d", p=P)
-            nc.sync.dma_start(
-                out=q_rows[:, :, positions_of(n), :],
-                in_=qk_sb[:, 0:HEADS].rearrange("p h t i e -> p h t (i e)"),
+        def finish_k(n):
+            tiles = chunks[n][3]
+            inv_rms = three_steps.tile([P, GROUPS, tiles], F32)
+            nc.vector.reciprocal(out=inv_rms[:], in_=rms_tiles[n][:])
+            k_sb = three_steps.tile([P, HEADS, tiles, PAIRS, 2], F32)
+            nc.gpsimd.tensor_tensor(
+                out=k_sb[:],
+                in0=rotated_tiles[n][:, HEADS:GROUPS].rearrange("p h t e i -> p h t i e"),
+                in1=inv_rms[:, HEADS:GROUPS]
+                .unsqueeze(3)
+                .unsqueeze(4)
+                .to_broadcast([P, HEADS, tiles, PAIRS, 2]),
+                op=ALU.mult,
             )
             nc.sync.dma_start(
-                out=k_rows[:, :, positions_of(n), :],
-                in_=qk_sb[:, HEADS:GROUPS].rearrange("p h t i e -> p h t (i e)"),
+                out=rows_of(out_1, n), in_=k_sb[:].rearrange("p h t i e -> p h t (i e)")
+            )
+            inv_rms_tiles[n] = inv_rms
+
+        def finish_q(n):
+            tiles = chunks[n][3]
+            q_sb = three_steps.tile([P, HEADS, tiles, PAIRS, 2], F32)
+            for h in range(HEADS):
+                for t in range(tiles):
+                    nc.scalar.activation(
+                        out=q_sb[:, h, t],
+                        in_=rotated_tiles[n][:, h, t].rearrange("p e i -> p i e"),
+                        func=ACT.Copy,
+                        scale=inv_rms_tiles[n][:, h, t : t + 1],
+                    )
+            nc.sync.dma_start(
+                out=rows_of(out_0, n), in_=q_sb[:].rearrange("p h t i e -> p h t (i e)")
             )
 
         load(0)
+        load(1)
         identity = consts.tile([P, P], F32)
         make_identity(nc, identity[:])
 
@@ -233,15 +290,45 @@ def tile_selfattention_pa_t_kernel(
                 .bitcast(I32),
             )
 
-        bias_row = consts.tile([P, 3 * STREAM], BF16)
-        nc.scalar.dma_start(out=bias_row[:], in_=qkv_b.partition_broadcast(P))
         gain_row = consts.tile([P, 2, HEAD_DIM], BF16)
         nc.scalar.dma_start(out=gain_row[:, 0, :], in_=q_scale.partition_broadcast(P))
         nc.scalar.dma_start(out=gain_row[:, 1, :], in_=k_scale.partition_broadcast(P))
         pe_rows = consts.tile([P, POS, 4 * PAIRS], BF16)
-        nc.scalar.dma_start(
-            out=pe_rows[:], in_=pe[0, 0].rearrange("(p j) i r c -> p j (i r c)", p=P)
-        )
+        pe_source = pe[0, 0].rearrange("(p j) i r c -> p j (i r c)", p=P)
+        nc.scalar.dma_start(out=pe_rows[:, 0:TILES, :], in_=pe_source[:, 0:TILES, :])
+        bias_row = consts.tile([P, 3 * STREAM], BF16)
+        nc.scalar.dma_start(out=bias_row[:], in_=qkv_b.partition_broadcast(P))
+        nc.scalar.dma_start(out=pe_rows[:, TILES:POS, :], in_=pe_source[:, TILES:POS, :])
+
+        own = consts.tile([P, QUARTERS, 2, TILES, 2, PAIRS], F32)
+        other = consts.tile([P, QUARTERS, 2, 2, TILES, PAIRS], F32)
+        pe_entry = pe_rows[:].rearrange("p (a t) (i r c) -> p a t i r c", t=TILES, r=2, c=2)
+        gain_entry = gain_row[:].rearrange("p s (i e) -> p s i e", e=2)
+
+        def make_tables(engine, begin, end):
+            for s in range(2):
+                for e in range(2):
+                    engine.tensor_tensor(
+                        out=own[:, begin:end, s, :, e, :],
+                        in0=pe_entry[:, begin:end, :, :, e, e],
+                        in1=gain_entry[:, s, :, e]
+                        .unsqueeze(1)
+                        .unsqueeze(2)
+                        .to_broadcast([P, end - begin, TILES, PAIRS]),
+                        op=ALU.mult,
+                    )
+                    engine.tensor_tensor(
+                        out=other[:, begin:end, s, e, :, :],
+                        in0=pe_entry[:, begin:end, :, :, e, 1 - e],
+                        in1=gain_entry[:, s, :, 1 - e]
+                        .unsqueeze(1)
+                        .unsqueeze(2)
+                        .to_broadcast([P, end - begin, TILES, PAIRS]),
+                        op=ALU.mult,
+                    )
+
+        make_tables(nc.vector, 0, 1)
+        make_tables(nc.gpsimd, 1, QUARTERS)
 
         bias_qk = consts.tile([P, GROUPS, 2, PAIRS], F32)
         nc.vector.tensor_copy(
@@ -253,38 +340,23 @@ def tile_selfattention_pa_t_kernel(
             out=bias_v[:], in_=bias_row[:, 2 * STREAM :].rearrange("p (h d) -> p h d", h=HEADS)
         )
 
-        own = consts.tile([P, 2, POS, 2, PAIRS], F32)
-        other = consts.tile([P, 2, 2, POS, PAIRS], F32)
-        pe_entry = pe_rows[:].rearrange("p j (i r c) -> p j i r c", r=2, c=2)
-        gain_entry = gain_row[:].rearrange("p s (i e) -> p s i e", e=2)
-        for s in range(2):
-            for e in range(2):
-                nc.gpsimd.tensor_tensor(
-                    out=own[:, s, :, e, :],
-                    in0=pe_entry[:, :, :, e, e],
-                    in1=gain_entry[:, s, :, e].unsqueeze(1).to_broadcast([P, POS, PAIRS]),
-                    op=ALU.mult,
-                )
-                nc.gpsimd.tensor_tensor(
-                    out=other[:, s, e, :, :],
-                    in0=pe_entry[:, :, :, e, 1 - e],
-                    in1=gain_entry[:, s, :, 1 - e].unsqueeze(1).to_broadcast([P, POS, PAIRS]),
-                    op=ALU.mult,
-                )
-
-        load(1)
-        for step in range(-2, n_chunks + 1):
-            if exists(step + 4):
-                load(step + 4)
-            if exists(step + 2):
-                turn(step + 2)
+        for step in range(-3, len(chunks) + 1):
+            if exists(step + 5):
+                load(step + 5)
+            if exists(step + 3):
+                turn(step + 3)
             if exists(step + 1):
                 project(step + 1)
+                if opens_quarter(step + 1):
+                    place_tables(chunks[step + 1][0])
             if exists(step):
                 add_bias(step)
-                measure(step)
-                rotate(step)
+            if exists(step - 1):
+                finish_k(step - 1)
             if exists(step + 2):
                 quantise(step + 2)
+            if exists(step):
+                measure(step)
+                rotate(step)
             if exists(step - 1):
-                finish(step - 1)
+                finish_q(step - 1)

@@ -23,8 +23,8 @@ PASSES = DIM // K_PASS
 WORDS = K_PASS // 2
 POS = SEQ // P
 TILES = 4
-QUARTERS = POS // TILES
 GROUPS = 2 * HEADS
+GPSIMD_TILES = 3
 
 FLOPS = 2 * BATCH * SEQ * DIM * 3 * STREAM
 
@@ -36,36 +36,25 @@ def tile_selfattention_pa_t_kernel(
     with ExitStack() as ctx:
         ctx.enter_context(tc.manual_schedule())
         consts = ctx.enter_context(tc.tile_pool(name="consts", bufs=1))
-        x_pool = ctx.enter_context(tc.tile_pool(name="x_pool", bufs=5))
+        x_pool = ctx.enter_context(tc.tile_pool(name="x_pool", bufs=4))
         two_steps = ctx.enter_context(tc.tile_pool(name="two_steps", bufs=2))
         three_steps = ctx.enter_context(tc.tile_pool(name="three_steps", bufs=3))
-        turn_psum = ctx.enter_context(tc.psum_pool(name="turn_psum", bufs=3))
-        qk_psum = ctx.enter_context(tc.psum_pool(name="qk_psum", bufs=2))
+        turn_psum = ctx.enter_context(tc.psum_pool(name="turn_psum", bufs=4))
+        qk_psum = ctx.enter_context(tc.psum_pool(name="qk_psum", bufs=3))
         v_psum = ctx.enter_context(tc.psum_pool(name="v_psum", bufs=1))
-        table_psum = ctx.enter_context(tc.psum_pool(name="table_psum", bufs=1))
 
-        chunks = [(0, 0, 0, 1), (0, 0, 1, 1), (0, 0, 2, 2)]
-        for quarter in range(QUARTERS):
-            for b in range(BATCH):
-                if 0 < quarter * BATCH + b < QUARTERS * BATCH - 1:
-                    chunks.append((quarter, b, 0, TILES))
-        chunks.extend(
-            [
-                (QUARTERS - 1, BATCH - 1, 0, 2),
-                (QUARTERS - 1, BATCH - 1, 2, 1),
-                (QUARTERS - 1, BATCH - 1, 3, 1),
-            ]
-        )
+        chunks = [(0, 0, 1), (0, 1, 1), (0, 2, 2)]
+        for b in range(BATCH):
+            for start in range(0, POS, TILES):
+                if 0 < b * POS + start < BATCH * POS - TILES:
+                    chunks.append((b, start, TILES))
+        chunks.extend([(BATCH - 1, POS - 4, 2), (BATCH - 1, POS - 2, 1), (BATCH - 1, POS - 1, 1)])
 
         def exists(n):
             return 0 <= n < len(chunks)
 
-        def opens_quarter(n):
-            return n == 0 or chunks[n][0] != chunks[n - 1][0]
-
         def rows_of(out, n):
-            quarter, b, first, tiles = chunks[n]
-            start = quarter * TILES + first
+            b, start, tiles = chunks[n]
             return out[b].rearrange("h (p j) d -> p h j d", p=P)[:, :, start : start + tiles, :]
 
         x_tiles = {}
@@ -76,11 +65,9 @@ def tile_selfattention_pa_t_kernel(
         rms_tiles = {}
         rotated_tiles = {}
         inv_rms_tiles = {}
-        table_banks = {}
 
         def load(n):
-            quarter, b, first, tiles = chunks[n]
-            start = quarter * TILES + first
+            b, start, tiles = chunks[n]
             x_sb = x_pool.tile([P, tiles, DIM], BF16)
             nc.sync.dma_start(
                 out=x_sb[:],
@@ -89,7 +76,7 @@ def tile_selfattention_pa_t_kernel(
             x_tiles[n] = x_sb
 
         def turn(n):
-            tiles = chunks[n][3]
+            tiles = chunks[n][2]
             grouped = two_steps.tile([P, tiles, PASSES, P, 4], BF16, align_bytes=64)
             for t in range(tiles):
                 x_words = x_tiles[n][:, t, :].bitcast(F32)
@@ -111,7 +98,7 @@ def tile_selfattention_pa_t_kernel(
             grouped_tiles[n] = grouped
 
         def quantise(n):
-            tiles = chunks[n][3]
+            tiles = chunks[n][2]
             x_codes = two_steps.tile([P, tiles, PASSES, P], U32, align_bytes=64)
             x_scales = two_steps.tile([P, tiles, PASSES, P], U8, align_bytes=64)
             nc.vector.quantize_mx(
@@ -122,7 +109,7 @@ def tile_selfattention_pa_t_kernel(
             code_tiles[n] = (x_codes, x_scales)
 
         def project(n):
-            tiles = chunks[n][3]
+            tiles = chunks[n][2]
             x_codes, x_scales = code_tiles[n]
             qk_banks = []
             for pair in range((tiles + 1) // 2):
@@ -147,27 +134,8 @@ def tile_selfattention_pa_t_kernel(
                         )
             banks[n] = (qk_banks, v_bank)
 
-        def place_tables(quarter):
-            own_bank = table_psum.tile([P, 2, TILES, HEAD_DIM], F32)
-            nc.tensor.matmul(
-                out=own_bank[:].rearrange("p s t d -> p (s t d)"),
-                lhsT=identity[:],
-                rhs=own[:, quarter].rearrange("p s t e i -> p (s t e i)"),
-                start=True,
-                stop=True,
-            )
-            other_bank = table_psum.tile([P, 2, 2, TILES, PAIRS], F32)
-            nc.tensor.matmul(
-                out=other_bank[:].rearrange("p s e t i -> p (s e t i)"),
-                lhsT=identity[:],
-                rhs=other[:, quarter].rearrange("p s e t i -> p (s e t i)"),
-                start=True,
-                stop=True,
-            )
-            table_banks[quarter] = (own_bank, other_bank)
-
         def add_bias(n):
-            tiles = chunks[n][3]
+            tiles = chunks[n][2]
             qk_banks, v_bank = banks[n]
             planes = two_steps.tile([P, GROUPS, tiles, 2, PAIRS], F32)
             for pair in range((tiles + 1) // 2):
@@ -193,7 +161,7 @@ def tile_selfattention_pa_t_kernel(
             plane_tiles[n] = planes
 
         def measure(n):
-            tiles = chunks[n][3]
+            tiles = chunks[n][2]
             squares = two_steps.tile([P, GROUPS, tiles, 2, PAIRS], F32)
             sum_sq = two_steps.tile([P, GROUPS, tiles], F32)
             for c in range(GROUPS):
@@ -211,15 +179,14 @@ def tile_selfattention_pa_t_kernel(
             rms_tiles[n] = rms
 
         def rotate(n):
-            quarter, b, first, tiles = chunks[n]
+            b, start, tiles = chunks[n]
             planes = plane_tiles[n]
-            own_bank, other_bank = table_banks[quarter]
             rotated = three_steps.tile([P, GROUPS, tiles, 2, PAIRS], F32)
             nc.vector.tensor_tensor(
                 out=rotated[:].rearrange("p (s h) t e i -> p s h (t e i)", s=2),
                 in0=planes[:].rearrange("p (s h) t e i -> p s h (t e i)", s=2),
-                in1=own_bank[:, :, first : first + tiles, :]
-                .rearrange("p s t d -> p s (t d)")
+                in1=own[:, :, start : start + tiles, :, :]
+                .rearrange("p s t e i -> p s (t e i)")
                 .unsqueeze(2)
                 .to_broadcast([P, 2, HEADS, tiles * HEAD_DIM]),
                 op=ALU.mult,
@@ -229,46 +196,50 @@ def tile_selfattention_pa_t_kernel(
                 nc.vector.tensor_tensor(
                     out=partner[:, :, :, e, :].rearrange("p (s h) t i -> p s h t i", s=2),
                     in0=planes[:, :, :, 1 - e, :].rearrange("p (s h) t i -> p s h t i", s=2),
-                    in1=other_bank[:, :, e, first : first + tiles, :]
+                    in1=other[:, :, e, start : start + tiles, :]
                     .unsqueeze(2)
                     .to_broadcast([P, 2, HEADS, tiles, PAIRS]),
                     op=ALU.mult,
                 )
-            nc.gpsimd.tensor_tensor(out=rotated[:], in0=rotated[:], in1=partner[:], op=ALU.add)
+            shared = min(tiles, GPSIMD_TILES)
+            nc.gpsimd.tensor_tensor(
+                out=rotated[:, :, 0:shared],
+                in0=rotated[:, :, 0:shared],
+                in1=partner[:, :, 0:shared],
+                op=ALU.add,
+            )
+            if shared < tiles:
+                nc.vector.tensor_tensor(
+                    out=rotated[:, :, shared:tiles],
+                    in0=rotated[:, :, shared:tiles],
+                    in1=partner[:, :, shared:tiles],
+                    op=ALU.add,
+                )
             rotated_tiles[n] = rotated
 
-        def finish_k(n):
-            tiles = chunks[n][3]
-            inv_rms = three_steps.tile([P, GROUPS, tiles], F32)
+        def invert(n):
+            inv_rms = three_steps.tile([P, GROUPS, chunks[n][2]], F32)
             nc.vector.reciprocal(out=inv_rms[:], in_=rms_tiles[n][:])
-            k_sb = three_steps.tile([P, HEADS, tiles, PAIRS, 2], F32)
-            nc.gpsimd.tensor_tensor(
-                out=k_sb[:],
-                in0=rotated_tiles[n][:, HEADS:GROUPS].rearrange("p h t e i -> p h t i e"),
-                in1=inv_rms[:, HEADS:GROUPS]
-                .unsqueeze(3)
-                .unsqueeze(4)
-                .to_broadcast([P, HEADS, tiles, PAIRS, 2]),
-                op=ALU.mult,
-            )
-            nc.sync.dma_start(
-                out=rows_of(out_1, n), in_=k_sb[:].rearrange("p h t i e -> p h t (i e)")
-            )
             inv_rms_tiles[n] = inv_rms
 
-        def finish_q(n):
-            tiles = chunks[n][3]
-            q_sb = three_steps.tile([P, HEADS, tiles, PAIRS, 2], F32)
-            for h in range(HEADS):
+        def finish(n):
+            tiles = chunks[n][2]
+            qk_sb = three_steps.tile([P, GROUPS, tiles, PAIRS, 2], F32)
+            for c in range(GROUPS):
                 for t in range(tiles):
                     nc.scalar.activation(
-                        out=q_sb[:, h, t],
-                        in_=rotated_tiles[n][:, h, t].rearrange("p e i -> p i e"),
+                        out=qk_sb[:, c, t],
+                        in_=rotated_tiles[n][:, c, t].rearrange("p e i -> p i e"),
                         func=ACT.Copy,
-                        scale=inv_rms_tiles[n][:, h, t : t + 1],
+                        scale=inv_rms_tiles[n][:, c, t : t + 1],
                     )
             nc.sync.dma_start(
-                out=rows_of(out_0, n), in_=q_sb[:].rearrange("p h t i e -> p h t (i e)")
+                out=rows_of(out_0, n),
+                in_=qk_sb[:, 0:HEADS].rearrange("p h t i e -> p h t (i e)"),
+            )
+            nc.sync.dma_start(
+                out=rows_of(out_1, n),
+                in_=qk_sb[:, HEADS:GROUPS].rearrange("p h t i e -> p h t (i e)"),
             )
 
         load(0)
@@ -300,35 +271,31 @@ def tile_selfattention_pa_t_kernel(
         nc.scalar.dma_start(out=bias_row[:], in_=qkv_b.partition_broadcast(P))
         nc.scalar.dma_start(out=pe_rows[:, TILES:POS, :], in_=pe_source[:, TILES:POS, :])
 
-        own = consts.tile([P, QUARTERS, 2, TILES, 2, PAIRS], F32)
-        other = consts.tile([P, QUARTERS, 2, 2, TILES, PAIRS], F32)
-        pe_entry = pe_rows[:].rearrange("p (a t) (i r c) -> p a t i r c", t=TILES, r=2, c=2)
+        own = consts.tile([P, 2, POS, 2, PAIRS], F32)
+        other = consts.tile([P, 2, 2, POS, PAIRS], F32)
+        pe_entry = pe_rows[:].rearrange("p j (i r c) -> p j i r c", r=2, c=2)
         gain_entry = gain_row[:].rearrange("p s (i e) -> p s i e", e=2)
 
         def make_tables(engine, begin, end):
             for s in range(2):
                 for e in range(2):
                     engine.tensor_tensor(
-                        out=own[:, begin:end, s, :, e, :],
-                        in0=pe_entry[:, begin:end, :, :, e, e],
-                        in1=gain_entry[:, s, :, e]
-                        .unsqueeze(1)
-                        .unsqueeze(2)
-                        .to_broadcast([P, end - begin, TILES, PAIRS]),
+                        out=own[:, s, begin:end, e, :],
+                        in0=pe_entry[:, begin:end, :, e, e],
+                        in1=gain_entry[:, s, :, e].unsqueeze(1).to_broadcast([P, end - begin, PAIRS]),
                         op=ALU.mult,
                     )
                     engine.tensor_tensor(
-                        out=other[:, begin:end, s, e, :, :],
-                        in0=pe_entry[:, begin:end, :, :, e, 1 - e],
+                        out=other[:, s, e, begin:end, :],
+                        in0=pe_entry[:, begin:end, :, e, 1 - e],
                         in1=gain_entry[:, s, :, 1 - e]
                         .unsqueeze(1)
-                        .unsqueeze(2)
-                        .to_broadcast([P, end - begin, TILES, PAIRS]),
+                        .to_broadcast([P, end - begin, PAIRS]),
                         op=ALU.mult,
                     )
 
-        make_tables(nc.vector, 0, 1)
-        make_tables(nc.gpsimd, 1, QUARTERS)
+        make_tables(nc.vector, 0, TILES)
+        make_tables(nc.gpsimd, TILES, POS)
 
         bias_qk = consts.tile([P, GROUPS, 2, PAIRS], F32)
         nc.vector.tensor_copy(
@@ -340,23 +307,21 @@ def tile_selfattention_pa_t_kernel(
             out=bias_v[:], in_=bias_row[:, 2 * STREAM :].rearrange("p (h d) -> p h d", h=HEADS)
         )
 
-        for step in range(-3, len(chunks) + 1):
-            if exists(step + 5):
-                load(step + 5)
-            if exists(step + 3):
-                turn(step + 3)
+        for step in range(-2, len(chunks) + 1):
+            if exists(step + 4):
+                load(step + 4)
+            if exists(step + 2):
+                turn(step + 2)
             if exists(step + 1):
                 project(step + 1)
-                if opens_quarter(step + 1):
-                    place_tables(chunks[step + 1][0])
             if exists(step):
                 add_bias(step)
             if exists(step - 1):
-                finish_k(step - 1)
-            if exists(step + 2):
-                quantise(step + 2)
+                invert(step - 1)
             if exists(step):
                 measure(step)
                 rotate(step)
+            if exists(step + 2):
+                quantise(step + 2)
             if exists(step - 1):
-                finish_q(step - 1)
+                finish(step - 1)

@@ -24,7 +24,7 @@ WORDS = K_PASS // 2
 POS = SEQ // P
 TILES = 4
 GROUPS = 2 * HEADS
-GPSIMD_TILES = 3
+GPSIMD_COLUMNS = 152
 
 FLOPS = 2 * BATCH * SEQ * DIM * 3 * STREAM
 
@@ -62,7 +62,6 @@ def tile_selfattention_pa_t_kernel(
         code_tiles = {}
         banks = {}
         plane_tiles = {}
-        rms_tiles = {}
         rotated_tiles = {}
         inv_rms_tiles = {}
 
@@ -172,11 +171,15 @@ def tile_selfattention_pa_t_kernel(
                         func=ACT.Square,
                         accum_out=sum_sq[:, c, t : t + 1],
                     )
-            rms = two_steps.tile([P, GROUPS, tiles], F32)
+            inv_rms = three_steps.tile([P, GROUPS, tiles], F32)
             nc.scalar.activation(
-                out=rms[:], in_=sum_sq[:], func=ACT.Sqrt, scale=1.0 / HEAD_DIM, bias=EPS
+                out=inv_rms[:],
+                in_=sum_sq[:],
+                func=ACT.Abs_reciprocal_sqrt,
+                scale=1.0 / HEAD_DIM,
+                bias=EPS,
             )
-            rms_tiles[n] = rms
+            inv_rms_tiles[n] = inv_rms
 
         def rotate(n):
             b, start, tiles = chunks[n]
@@ -201,26 +204,25 @@ def tile_selfattention_pa_t_kernel(
                     .to_broadcast([P, 2, HEADS, tiles, PAIRS]),
                     op=ALU.mult,
                 )
-            shared = min(tiles, GPSIMD_TILES)
-            nc.gpsimd.tensor_tensor(
-                out=rotated[:, :, 0:shared],
-                in0=rotated[:, :, 0:shared],
-                in1=partner[:, :, 0:shared],
-                op=ALU.add,
-            )
-            if shared < tiles:
+            row = tiles * HEAD_DIM
+            shared = GPSIMD_COLUMNS if tiles == TILES else 0
+            sums = rotated[:].rearrange("p c t e i -> p c (t e i)")
+            terms = partner[:].rearrange("p c t e i -> p c (t e i)")
+            if shared > 0:
+                nc.gpsimd.tensor_tensor(
+                    out=sums[:, :, 0:shared],
+                    in0=sums[:, :, 0:shared],
+                    in1=terms[:, :, 0:shared],
+                    op=ALU.add,
+                )
+            if shared < row:
                 nc.vector.tensor_tensor(
-                    out=rotated[:, :, shared:tiles],
-                    in0=rotated[:, :, shared:tiles],
-                    in1=partner[:, :, shared:tiles],
+                    out=sums[:, :, shared:row],
+                    in0=sums[:, :, shared:row],
+                    in1=terms[:, :, shared:row],
                     op=ALU.add,
                 )
             rotated_tiles[n] = rotated
-
-        def invert(n):
-            inv_rms = three_steps.tile([P, GROUPS, chunks[n][2]], F32)
-            nc.vector.reciprocal(out=inv_rms[:], in_=rms_tiles[n][:])
-            inv_rms_tiles[n] = inv_rms
 
         def finish(n):
             tiles = chunks[n][2]
@@ -316,8 +318,6 @@ def tile_selfattention_pa_t_kernel(
                 project(step + 1)
             if exists(step):
                 add_bias(step)
-            if exists(step - 1):
-                invert(step - 1)
             if exists(step):
                 measure(step)
                 rotate(step)

@@ -24,7 +24,7 @@ WORDS = K_PASS // 2
 POS = SEQ // P
 TILES = 4
 GROUPS = 2 * HEADS
-GPSIMD_COLUMNS = 152
+GPSIMD_COLUMNS = 176
 
 FLOPS = 2 * BATCH * SEQ * DIM * 3 * STREAM
 
@@ -64,6 +64,7 @@ def tile_selfattention_pa_t_kernel(
         plane_tiles = {}
         rotated_tiles = {}
         inv_rms_tiles = {}
+        rest_of_sum = {}
 
         def load(n):
             b, start, tiles = chunks[n]
@@ -215,14 +216,12 @@ def tile_selfattention_pa_t_kernel(
                     in1=terms[:, :, 0:shared],
                     op=ALU.add,
                 )
-            if shared < row:
-                nc.vector.tensor_tensor(
-                    out=sums[:, :, shared:row],
-                    in0=sums[:, :, shared:row],
-                    in1=terms[:, :, shared:row],
-                    op=ALU.add,
-                )
             rotated_tiles[n] = rotated
+            rest_of_sum[n] = (sums[:, :, shared:row], terms[:, :, shared:row])
+
+        def add_rest(n):
+            sums_rest, terms_rest = rest_of_sum[n]
+            nc.vector.tensor_tensor(out=sums_rest, in0=sums_rest, in1=terms_rest, op=ALU.add)
 
         def finish(n):
             tiles = chunks[n][2]
@@ -323,5 +322,7 @@ def tile_selfattention_pa_t_kernel(
                 rotate(step)
             if exists(step + 2):
                 quantise(step + 2)
+            if exists(step):
+                add_rest(step)
             if exists(step - 1):
                 finish(step - 1)

@@ -24,7 +24,7 @@ WORDS = K_PASS // 2
 POS = SEQ // P
 TILES = 4
 GROUPS = 2 * HEADS
-GPSIMD_COLUMNS = 176
+GPSIMD_COLUMNS = 152
 
 FLOPS = 2 * BATCH * SEQ * DIM * 3 * STREAM
 
@@ -116,22 +116,22 @@ def tile_selfattention_pa_t_kernel(
                 qk_bank = qk_psum.tile([P, 2, 2, STREAM], F32)
                 qk_banks.append(qk_bank)
             v_bank = v_psum.tile([P, TILES, STREAM], F32)
-            for t in range(tiles):
-                for s in range(3):
-                    if s < 2:
-                        product = qk_banks[t // 2][:, t % 2, s, :]
-                    else:
-                        product = v_bank[:, t, :]
-                    for g in range(PASSES):
-                        nc.tensor.matmul_mx(
-                            out=product,
-                            lhsT=x_codes[:, t, g, :].bitcast(FP8X4),
-                            lhsT_scale=x_scales[:, t, g, :],
-                            rhs=w_words[:, g, 2 * STREAM * s : 2 * STREAM * (s + 1)].bitcast(FP4X4),
-                            rhs_scale=w_scales[:, g, STREAM * s : STREAM * (s + 1)],
-                            start=(g == 0),
-                            stop=(g == PASSES - 1),
-                        )
+            q_and_k = [(t, s) for t in range(tiles) for s in range(2)]
+            for t, s in q_and_k + [(t, 2) for t in range(tiles)]:
+                if s < 2:
+                    product = qk_banks[t // 2][:, t % 2, s, :]
+                else:
+                    product = v_bank[:, t, :]
+                for g in range(PASSES):
+                    nc.tensor.matmul_mx(
+                        out=product,
+                        lhsT=x_codes[:, t, g, :].bitcast(FP8X4),
+                        lhsT_scale=x_scales[:, t, g, :],
+                        rhs=w_words[:, g, 2 * STREAM * s : 2 * STREAM * (s + 1)].bitcast(FP4X4),
+                        rhs_scale=w_scales[:, g, STREAM * s : STREAM * (s + 1)],
+                        start=(g == 0),
+                        stop=(g == PASSES - 1),
+                    )
             banks[n] = (qk_banks, v_bank)
 
         def add_bias(n):
@@ -262,55 +262,53 @@ def tile_selfattention_pa_t_kernel(
                 .bitcast(I32),
             )
 
-        gain_row = consts.tile([P, 2, HEAD_DIM], BF16)
-        nc.scalar.dma_start(out=gain_row[:, 0, :], in_=q_scale.partition_broadcast(P))
-        nc.scalar.dma_start(out=gain_row[:, 1, :], in_=k_scale.partition_broadcast(P))
         pe_rows = consts.tile([P, POS, 4 * PAIRS], BF16)
         pe_source = pe[0, 0].rearrange("(p j) i r c -> p j (i r c)", p=P)
         nc.scalar.dma_start(out=pe_rows[:, 0:TILES, :], in_=pe_source[:, 0:TILES, :])
+        gain_row = consts.tile([P, 2, HEAD_DIM], BF16)
+        nc.scalar.dma_start(out=gain_row[:, 0, :], in_=q_scale.partition_broadcast(P))
+        nc.scalar.dma_start(out=gain_row[:, 1, :], in_=k_scale.partition_broadcast(P))
         bias_row = consts.tile([P, 3 * STREAM], BF16)
         nc.scalar.dma_start(out=bias_row[:], in_=qkv_b.partition_broadcast(P))
-        nc.scalar.dma_start(out=pe_rows[:, TILES:POS, :], in_=pe_source[:, TILES:POS, :])
 
         own = consts.tile([P, 2, POS, 2, PAIRS], F32)
         other = consts.tile([P, 2, 2, POS, PAIRS], F32)
         pe_entry = pe_rows[:].rearrange("p j (i r c) -> p j i r c", r=2, c=2)
         gain_entry = gain_row[:].rearrange("p s (i e) -> p s i e", e=2)
 
-        def make_tables(engine, begin, end):
-            for s in range(2):
-                for e in range(2):
-                    engine.tensor_tensor(
-                        out=own[:, s, begin:end, e, :],
-                        in0=pe_entry[:, begin:end, :, e, e],
-                        in1=gain_entry[:, s, :, e].unsqueeze(1).to_broadcast([P, end - begin, PAIRS]),
-                        op=ALU.mult,
-                    )
-                    engine.tensor_tensor(
-                        out=other[:, s, e, begin:end, :],
-                        in0=pe_entry[:, begin:end, :, e, 1 - e],
-                        in1=gain_entry[:, s, :, 1 - e]
-                        .unsqueeze(1)
-                        .to_broadcast([P, end - begin, PAIRS]),
-                        op=ALU.mult,
-                    )
-
-        make_tables(nc.vector, 0, TILES)
-        make_tables(nc.gpsimd, TILES, POS)
+        def make_tables(begin, end):
+            spread = [P, 2, end - begin, PAIRS]
+            for e in range(2):
+                nc.vector.tensor_tensor(
+                    out=own[:, :, begin:end, e, :],
+                    in0=pe_entry[:, begin:end, :, e, e].unsqueeze(1).to_broadcast(spread),
+                    in1=gain_entry[:, :, :, e].unsqueeze(2).to_broadcast(spread),
+                    op=ALU.mult,
+                )
+                nc.vector.tensor_tensor(
+                    out=other[:, :, e, begin:end, :],
+                    in0=pe_entry[:, begin:end, :, e, 1 - e].unsqueeze(1).to_broadcast(spread),
+                    in1=gain_entry[:, :, :, 1 - e].unsqueeze(2).to_broadcast(spread),
+                    op=ALU.mult,
+                )
 
         bias_qk = consts.tile([P, GROUPS, 2, PAIRS], F32)
-        nc.vector.tensor_copy(
-            out=bias_qk[:],
-            in_=bias_row[:, 0 : 2 * STREAM].rearrange("p (c i e) -> p c e i", c=GROUPS, e=2),
-        )
         bias_v = consts.tile([P, HEADS, HEAD_DIM], F32)
-        nc.vector.tensor_copy(
-            out=bias_v[:], in_=bias_row[:, 2 * STREAM :].rearrange("p (h d) -> p h d", h=HEADS)
-        )
+
+        def spread_bias():
+            nc.vector.tensor_copy(
+                out=bias_qk[:],
+                in_=bias_row[:, 0 : 2 * STREAM].rearrange("p (c i e) -> p c e i", c=GROUPS, e=2),
+            )
+            nc.vector.tensor_copy(
+                out=bias_v[:], in_=bias_row[:, 2 * STREAM :].rearrange("p (h d) -> p h d", h=HEADS)
+            )
 
         for step in range(-2, len(chunks) + 1):
             if exists(step + 4):
                 load(step + 4)
+            if step == -1:
+                nc.sync.dma_start(out=pe_rows[:, TILES:POS, :], in_=pe_source[:, TILES:POS, :])
             if exists(step + 2):
                 turn(step + 2)
             if exists(step + 1):
@@ -320,8 +318,13 @@ def tile_selfattention_pa_t_kernel(
             if exists(step):
                 measure(step)
                 rotate(step)
+            if step == 1:
+                make_tables(TILES, POS)
             if exists(step + 2):
                 quantise(step + 2)
+            if step == -2:
+                make_tables(0, TILES)
+                spread_bias()
             if exists(step):
                 add_rest(step)
             if exists(step - 1):

from contextlib import ExitStack

import concourse.mybir as mybir
from concourse.masks import make_identity

F32 = mybir.dt.float32
BF16 = mybir.dt.bfloat16
I32 = mybir.dt.int32
U32 = mybir.dt.uint32
U8 = mybir.dt.uint8
FP8X4 = mybir.dt.float8_e4m3fn_x4
FP4X4 = mybir.dt.float4_e2m1fn_x4
ALU = mybir.AluOpType
ACT = mybir.ActivationFunctionType

P = 128
BATCH, SEQ, DIM, HEADS, HEAD_DIM = 4, 2048, 1024, 2, 64
EPS = 1e-6
PAIRS = HEAD_DIM // 2
STREAM = HEADS * HEAD_DIM
K_PASS = 4 * P
PASSES = DIM // K_PASS
WORDS = K_PASS // 2
POS = SEQ // P
TILES = 4
GROUPS = 2 * HEADS
GPSIMD_COLUMNS = 152

FLOPS = 2 * BATCH * SEQ * DIM * 3 * STREAM


def tile_selfattention_pa_t_kernel(
    tc, x, pe, qkv_w_words, qkv_w_scales, qkv_b, q_scale, k_scale, out_0, out_1, out_2
):
    nc = tc.nc
    with ExitStack() as ctx:
        ctx.enter_context(tc.manual_schedule())
        consts = ctx.enter_context(tc.tile_pool(name="consts", bufs=1))
        x_pool = ctx.enter_context(tc.tile_pool(name="x_pool", bufs=4))
        two_steps = ctx.enter_context(tc.tile_pool(name="two_steps", bufs=2))
        three_steps = ctx.enter_context(tc.tile_pool(name="three_steps", bufs=3))
        turn_psum = ctx.enter_context(tc.psum_pool(name="turn_psum", bufs=4))
        qk_psum = ctx.enter_context(tc.psum_pool(name="qk_psum", bufs=3))
        v_psum = ctx.enter_context(tc.psum_pool(name="v_psum", bufs=1))

        chunks = [(0, 0, 1), (0, 1, 1), (0, 2, 2)]
        for b in range(BATCH):
            for start in range(0, POS, TILES):
                if 0 < b * POS + start < BATCH * POS - TILES:
                    chunks.append((b, start, TILES))
        chunks.extend([(BATCH - 1, POS - 4, 2), (BATCH - 1, POS - 2, 1), (BATCH - 1, POS - 1, 1)])

        def exists(n):
            return 0 <= n < len(chunks)

        def rows_of(out, n):
            b, start, tiles = chunks[n]
            return out[b].rearrange("h (p j) d -> p h j d", p=P)[:, :, start : start + tiles, :]

        x_tiles = {}
        grouped_tiles = {}
        code_tiles = {}
        banks = {}
        plane_tiles = {}
        rotated_tiles = {}
        inv_rms_tiles = {}
        rest_of_sum = {}

        def load(n):
            b, start, tiles = chunks[n]
            x_sb = x_pool.tile([P, tiles, DIM], BF16)
            nc.sync.dma_start(
                out=x_sb[:],
                in_=x[b].rearrange("(p j) k -> p j k", p=P)[:, start : start + tiles, :],
            )
            x_tiles[n] = x_sb

        def turn(n):
            tiles = chunks[n][2]
            grouped = two_steps.tile([P, tiles, PASSES, P, 4], BF16, align_bytes=64)
            for t in range(tiles):
                x_words = x_tiles[n][:, t, :].bitcast(F32)
                turned = turn_psum.tile([P, PASSES, 2, P], F32)
                for g in range(PASSES):
                    for u in range(2):
                        nc.tensor.transpose(
                            turned[:, g, u, :],
                            x_words[:, WORDS * g + u : WORDS * (g + 1) : 2],
                            identity[:],
                        )
                nc.scalar.copy(
                    out=grouped[:, t]
                    .rearrange("p g r k -> p g (r k)")
                    .bitcast(F32)
                    .rearrange("p g (r u) -> p g r u", u=2),
                    in_=turned[:].rearrange("p g u r -> p g r u"),
                )
            grouped_tiles[n] = grouped

        def quantise(n):
            tiles = chunks[n][2]
            x_codes = two_steps.tile([P, tiles, PASSES, P], U32, align_bytes=64)
            x_scales = two_steps.tile([P, tiles, PASSES, P], U8, align_bytes=64)
            nc.vector.quantize_mx(
                out=x_codes[:].rearrange("p t g r -> p (t g r)").bitcast(FP8X4),
                scales=x_scales[:].rearrange("p t g r -> p (t g r)"),
                in_=grouped_tiles[n][:].rearrange("p t g r k -> p (t g r k)"),
            )
            code_tiles[n] = (x_codes, x_scales)

        def project(n):
            tiles = chunks[n][2]
            x_codes, x_scales = code_tiles[n]
            qk_banks = []
            for pair in range((tiles + 1) // 2):
                qk_bank = qk_psum.tile([P, 2, 2, STREAM], F32)
                qk_banks.append(qk_bank)
            v_bank = v_psum.tile([P, TILES, STREAM], F32)
            q_and_k = [(t, s) for t in range(tiles) for s in range(2)]
            for t, s in q_and_k + [(t, 2) for t in range(tiles)]:
                if s < 2:
                    product = qk_banks[t // 2][:, t % 2, s, :]
                else:
                    product = v_bank[:, t, :]
                for g in range(PASSES):
                    nc.tensor.matmul_mx(
                        out=product,
                        lhsT=x_codes[:, t, g, :].bitcast(FP8X4),
                        lhsT_scale=x_scales[:, t, g, :],
                        rhs=w_words[:, g, 2 * STREAM * s : 2 * STREAM * (s + 1)].bitcast(FP4X4),
                        rhs_scale=w_scales[:, g, STREAM * s : STREAM * (s + 1)],
                        start=(g == 0),
                        stop=(g == PASSES - 1),
                    )
            banks[n] = (qk_banks, v_bank)

        def add_bias(n):
            tiles = chunks[n][2]
            qk_banks, v_bank = banks[n]
            planes = two_steps.tile([P, GROUPS, tiles, 2, PAIRS], F32)
            for pair in range((tiles + 1) // 2):
                held = min(2, tiles - 2 * pair)
                nc.vector.tensor_tensor(
                    out=planes[:, :, 2 * pair : 2 * pair + held, :, :].rearrange(
                        "p c t e i -> p t c e i"
                    ),
                    in0=qk_banks[pair][:, 0:held].rearrange(
                        "p t s (h i e) -> p t (s h) e i", h=HEADS, e=2
                    ),
                    in1=bias_qk[:].unsqueeze(1).to_broadcast([P, held, GROUPS, 2, PAIRS]),
                    op=ALU.add,
                )
            v_sb = three_steps.tile([P, HEADS, tiles, HEAD_DIM], F32)
            nc.vector.tensor_tensor(
                out=v_sb[:].rearrange("p h t d -> p t h d"),
                in0=v_bank[:, 0:tiles, :].rearrange("p t (h d) -> p t h d", h=HEADS),
                in1=bias_v[:].unsqueeze(1).to_broadcast([P, tiles, HEADS, HEAD_DIM]),
                op=ALU.add,
            )
            nc.sync.dma_start(out=rows_of(out_2, n), in_=v_sb[:])
            plane_tiles[n] = planes

        def measure(n):
            tiles = chunks[n][2]
            squares = two_steps.tile([P, GROUPS, tiles, 2, PAIRS], F32)
            sum_sq = two_steps.tile([P, GROUPS, tiles], F32)
            for c in range(GROUPS):
                for t in range(tiles):
                    nc.scalar.activation(
                        out=squares[:, c, t],
                        in_=plane_tiles[n][:, c, t],
                        func=ACT.Square,
                        accum_out=sum_sq[:, c, t : t + 1],
                    )
            inv_rms = three_steps.tile([P, GROUPS, tiles], F32)
            nc.scalar.activation(
                out=inv_rms[:],
                in_=sum_sq[:],
                func=ACT.Abs_reciprocal_sqrt,
                scale=1.0 / HEAD_DIM,
                bias=EPS,
            )
            inv_rms_tiles[n] = inv_rms

        def rotate(n):
            b, start, tiles = chunks[n]
            planes = plane_tiles[n]
            rotated = three_steps.tile([P, GROUPS, tiles, 2, PAIRS], F32)
            nc.vector.tensor_tensor(
                out=rotated[:].rearrange("p (s h) t e i -> p s h (t e i)", s=2),
                in0=planes[:].rearrange("p (s h) t e i -> p s h (t e i)", s=2),
                in1=own[:, :, start : start + tiles, :, :]
                .rearrange("p s t e i -> p s (t e i)")
                .unsqueeze(2)
                .to_broadcast([P, 2, HEADS, tiles * HEAD_DIM]),
                op=ALU.mult,
            )
            partner = two_steps.tile([P, GROUPS, tiles, 2, PAIRS], F32)
            for e in range(2):
                nc.vector.tensor_tensor(
                    out=partner[:, :, :, e, :].rearrange("p (s h) t i -> p s h t i", s=2),
                    in0=planes[:, :, :, 1 - e, :].rearrange("p (s h) t i -> p s h t i", s=2),
                    in1=other[:, :, e, start : start + tiles, :]
                    .unsqueeze(2)
                    .to_broadcast([P, 2, HEADS, tiles, PAIRS]),
                    op=ALU.mult,
                )
            row = tiles * HEAD_DIM
            shared = GPSIMD_COLUMNS if tiles == TILES else 0
            sums = rotated[:].rearrange("p c t e i -> p c (t e i)")
            terms = partner[:].rearrange("p c t e i -> p c (t e i)")
            if shared > 0:
                nc.gpsimd.tensor_tensor(
                    out=sums[:, :, 0:shared],
                    in0=sums[:, :, 0:shared],
                    in1=terms[:, :, 0:shared],
                    op=ALU.add,
                )
            rotated_tiles[n] = rotated
            rest_of_sum[n] = (sums[:, :, shared:row], terms[:, :, shared:row])

        def add_rest(n):
            sums_rest, terms_rest = rest_of_sum[n]
            nc.vector.tensor_tensor(out=sums_rest, in0=sums_rest, in1=terms_rest, op=ALU.add)

        def finish(n):
            tiles = chunks[n][2]
            qk_sb = three_steps.tile([P, GROUPS, tiles, PAIRS, 2], F32)
            for c in range(GROUPS):
                for t in range(tiles):
                    nc.scalar.activation(
                        out=qk_sb[:, c, t],
                        in_=rotated_tiles[n][:, c, t].rearrange("p e i -> p i e"),
                        func=ACT.Copy,
                        scale=inv_rms_tiles[n][:, c, t : t + 1],
                    )
            nc.sync.dma_start(
                out=rows_of(out_0, n),
                in_=qk_sb[:, 0:HEADS].rearrange("p h t i e -> p h t (i e)"),
            )
            nc.sync.dma_start(
                out=rows_of(out_1, n),
                in_=qk_sb[:, HEADS:GROUPS].rearrange("p h t i e -> p h t (i e)"),
            )

        load(0)
        load(1)
        identity = consts.tile([P, P], F32)
        make_identity(nc, identity[:])

        w_words = consts.tile([P, PASSES, 2 * 3 * STREAM], U8, align_bytes=64)
        nc.sync.dma_start(
            out=w_words[:].bitcast(I32), in_=qkv_w_words.rearrange("g p n -> p g n").bitcast(I32)
        )
        w_scales = consts.tile([P, PASSES, 3 * STREAM], U8, align_bytes=64)
        nc.vector.memset(w_scales[:].rearrange("p g n -> p (g n)").bitcast(I32), 0)
        for quadrant in range(4):
            nc.sync.dma_start(
                out=w_scales[32 * quadrant : 32 * quadrant + 4, :, :].bitcast(I32),
                in_=qkv_w_scales[:, 4 * quadrant : 4 * quadrant + 4, :]
                .rearrange("g r n -> r g n")
                .bitcast(I32),
            )

        pe_rows = consts.tile([P, POS, 4 * PAIRS], BF16)
        pe_source = pe[0, 0].rearrange("(p j) i r c -> p j (i r c)", p=P)
        nc.scalar.dma_start(out=pe_rows[:, 0:TILES, :], in_=pe_source[:, 0:TILES, :])
        gain_row = consts.tile([P, 2, HEAD_DIM], BF16)
        nc.scalar.dma_start(out=gain_row[:, 0, :], in_=q_scale.partition_broadcast(P))
        nc.scalar.dma_start(out=gain_row[:, 1, :], in_=k_scale.partition_broadcast(P))
        bias_row = consts.tile([P, 3 * STREAM], BF16)
        nc.scalar.dma_start(out=bias_row[:], in_=qkv_b.partition_broadcast(P))

        own = consts.tile([P, 2, POS, 2, PAIRS], F32)
        other = consts.tile([P, 2, 2, POS, PAIRS], F32)
        pe_entry = pe_rows[:].rearrange("p j (i r c) -> p j i r c", r=2, c=2)
        gain_entry = gain_row[:].rearrange("p s (i e) -> p s i e", e=2)

        def make_tables(begin, end):
            spread = [P, 2, end - begin, PAIRS]
            for e in range(2):
                nc.vector.tensor_tensor(
                    out=own[:, :, begin:end, e, :],
                    in0=pe_entry[:, begin:end, :, e, e].unsqueeze(1).to_broadcast(spread),
                    in1=gain_entry[:, :, :, e].unsqueeze(2).to_broadcast(spread),
                    op=ALU.mult,
                )
                nc.vector.tensor_tensor(
                    out=other[:, :, e, begin:end, :],
                    in0=pe_entry[:, begin:end, :, e, 1 - e].unsqueeze(1).to_broadcast(spread),
                    in1=gain_entry[:, :, :, 1 - e].unsqueeze(2).to_broadcast(spread),
                    op=ALU.mult,
                )

        bias_qk = consts.tile([P, GROUPS, 2, PAIRS], F32)
        bias_v = consts.tile([P, HEADS, HEAD_DIM], F32)

        def spread_bias():
            nc.vector.tensor_copy(
                out=bias_qk[:],
                in_=bias_row[:, 0 : 2 * STREAM].rearrange("p (c i e) -> p c e i", c=GROUPS, e=2),
            )
            nc.vector.tensor_copy(
                out=bias_v[:], in_=bias_row[:, 2 * STREAM :].rearrange("p (h d) -> p h d", h=HEADS)
            )

        for step in range(-2, len(chunks) + 1):
            if exists(step + 4):
                load(step + 4)
            if step == -1:
                nc.sync.dma_start(out=pe_rows[:, TILES:POS, :], in_=pe_source[:, TILES:POS, :])
            if exists(step + 2):
                turn(step + 2)
            if exists(step + 1):
                project(step + 1)
            if exists(step):
                add_bias(step)
            if exists(step):
                measure(step)
                rotate(step)
            if step == 1:
                make_tables(TILES, POS)
            if exists(step + 2):
                quantise(step + 2)
            if step == -2:
                make_tables(0, TILES)
                spread_bias()
            if exists(step):
                add_rest(step)
            if exists(step - 1):
                finish(step - 1)
